import numpy as np
import ml_dtypes


def mxq(x, axis, fmt="e4m3"):
    dtype, down = {"e4m3": (ml_dtypes.float8_e4m3fn, 7), "e5m2": (ml_dtypes.float8_e5m2, 14)}[fmt]
    v = np.moveaxis(np.asarray(x, np.float32).astype(ml_dtypes.bfloat16).astype(np.float64), axis, -1)
    blocks = v.reshape(v.shape[:-1] + (-1, 32))
    amax = np.abs(blocks).max(-1, keepdims=True)
    byte = np.maximum(np.where(amax > 0, np.frexp(amax)[1] - 1 + 127, 0) - down, 1)
    scale = np.exp2(byte - 127.0)
    codes = (blocks / scale).astype(np.float32).astype(dtype).astype(np.float64)
    return np.moveaxis((codes * scale).reshape(v.shape), -1, axis)


WIDE = False


def mx_kscale(k):
    if not WIDE:
        return np.ones(k)
    levels = np.array([10, -10, 5, -5, 0])
    a = np.random.permutation(np.resize(levels, k // 512 * 4)).reshape(k // 512, 4)
    idx = np.arange(k)
    return np.exp2(a[idx // 512, idx % 128 // 32])


BF16 = ml_dtypes.bfloat16


def bf(x):
    return np.asarray(x, np.float32).astype(BF16)


def f64(x):
    return np.asarray(x).astype(np.float64)


M, K, P, Q = 8192, 1024, 8, 16
N = P * Q
SCALING = 2.0


def _kron(A, B):
    m, n = A.shape
    p, q = B.shape
    return (A[:, None, :, None] * B[None, :, None, :]).reshape(m * p, n * q)


def setup_inputs():
    s = mx_kscale(K)
    return {"x": bf(np.random.standard_normal((M, K)) * s),
            "original_weight": bf(np.random.standard_normal((N, K)) / np.sqrt(K) / s),
            "lokr_A": bf(np.random.standard_normal((P, K)) / np.sqrt(K) / s),
            "lokr_B": bf(np.random.standard_normal((Q, 1)) * 0.25),
            "scalar": bf(1.5 + 0.1 * np.random.standard_normal(1))}


def reference(x, original_weight, lokr_A, lokr_B, scalar):
    delta_W = _kron(f64(lokr_A), f64(lokr_B)) * SCALING
    W_eff = f64(original_weight) + f64(scalar)[0] * delta_W
    return mxq(f64(x), 1, "e4m3") @ mxq(W_eff, 1, "e4m3").T

@@ -1,0 +1,228 @@
+from contextlib import ExitStack
+
+import concourse.mybir as mybir
+from concourse.masks import make_identity
+
+F32 = mybir.dt.float32
+BF16 = mybir.dt.bfloat16
+U32 = mybir.dt.uint32
+U8 = mybir.dt.uint8
+I32 = mybir.dt.int32
+FP8X4 = mybir.dt.float8_e4m3fn_x4
+ADD = mybir.AluOpType.add
+MULT = mybir.AluOpType.mult
+
+P = 128
+M_ROWS = 8192
+K = 1024
+N_OUT = 128
+N_TILES = M_ROWS // P
+ROUND = 4
+N_ROUNDS = N_TILES // ROUND
+XT_BANKS = 6
+LOAD_CHUNKS = [1, 1, 2, 4, 8, 8, 8, 8, 8, 8, 4, 4]
+STORE_GROUPS = [16, 16, 16, 8, 4, 4]
+SCALING = 2.0
+
+FLOPS = 2 * M_ROWS * K * N_OUT
+
+
+def tile_lokrlayer_t_kernel(tc, x, original_weight, lokr_A, lokr_B, scalar, out):
+    nc = tc.nc
+    x_v = x.rearrange("(p t) k -> p t k", t=N_TILES)
+    out_v = out.rearrange("(p t) n -> p t n", t=N_TILES)
+
+    with ExitStack() as ctx:
+        consts = ctx.enter_context(tc.tile_pool(name="consts", bufs=1))
+        xpool = ctx.enter_context(tc.tile_pool(name="xpool", bufs=1))
+        opool = ctx.enter_context(tc.tile_pool(name="opool", bufs=1))
+        work = ctx.enter_context(tc.tile_pool(name="work", bufs=3))
+        psum = ctx.enter_context(tc.psum_pool(name="psum", bufs=1))
+        ctx.enter_context(tc.manual_schedule())
+
+        par = consts.tile([P, K + 64], BF16, name="par")
+        nc.vector.memset(par[:].bitcast(I32), 0)
+        ident_f = consts.tile([P, P], F32, name="ident_f")
+        make_identity(nc, ident_f[:])
+
+        x_words = []
+        x_tiles = []
+        t0 = 0
+        for c, width in enumerate(LOAD_CHUNKS):
+            xs = xpool.tile([P, width * K], BF16, name="x%d" % c)
+            x_tiles.append((xs, t0, width))
+            xw = xs[:].bitcast(F32)
+            for j in range(width):
+                x_words.append((xw, j * (K // 2)))
+            t0 += width
+
+        def load(c):
+            xs, first, width = x_tiles[c]
+            nc.sync.dma_start(
+                out=xs[:], in_=x_v[:, first : first + width, :].rearrange("p t k -> p (t k)")
+            )
+
+        for c in range(4):
+            load(c)
+
+        ow = consts.tile([P, K], BF16, name="ow")
+        nc.scalar.dma_start(out=par[0:8, 0:K], in_=lokr_A)
+        nc.scalar.dma_start(out=par[8:24, K : K + 1], in_=lokr_B)
+        nc.scalar.dma_start(out=par[24:25, K + 1 : K + 2], in_=scalar.unsqueeze(0))
+        nc.scalar.dma_start(out=ow[:], in_=original_weight)
+
+        for c in range(4, len(LOAD_CHUNKS)):
+            load(c)
+
+        sel = consts.tile([P, 8, 16], BF16, name="sel")
+        nc.vector.scalar_tensor_tensor(
+            out=sel[:],
+            in0=ident_f[:, 0:8].unsqueeze(2).to_broadcast([P, 8, 16]),
+            scalar=ident_f[:, 24:25],
+            in1=ident_f[:, 8:24].unsqueeze(1).to_broadcast([P, 8, 16]),
+            op0=ADD,
+            op1=ADD,
+        )
+        ident_b = consts.tile([P, P], BF16, name="ident_b")
+        nc.vector.tensor_copy(out=ident_b[:], in_=ident_f[:])
+        sel2 = sel[:].rearrange("p a b -> p (a b)")
+
+        small = psum.tile([P, 512], F32, tag="acc0", name="small")
+        nc.tensor.matmul(small[:, 0:64], lhsT=sel2, rhs=par[:, K : K + 64], start=True, stop=True)
+        arep1 = psum.tile([P, 512], F32, tag="acc1", name="arep1")
+        nc.tensor.matmul(arep1[:], lhsT=sel2, rhs=par[:, 512:1024], start=True, stop=True)
+        cs = consts.tile([P, 2], F32, name="cs")
+        nc.vector.tensor_copy(out=cs[:], in_=small[:, 0:2])
+        arep0 = psum.tile([P, 512], F32, tag="acc0", name="arep0")
+        nc.tensor.matmul(arep0[:], lhsT=sel2, rhs=par[:, 0:512], start=True, stop=True)
+        gain = consts.tile([P, 1], F32, name="gain")
+        nc.vector.tensor_scalar(
+            out=gain[:], in0=cs[:, 0:1], scalar1=cs[:, 1:2], scalar2=SCALING, op0=MULT, op1=MULT
+        )
+        w_d = consts.tile([P, 2, 2, 256], BF16, name="w_d")
+        arep = [arep0, arep1]
+        for g in (1, 0):
+            nc.vector.scalar_tensor_tensor(
+                out=w_d[:, :, g, :],
+                in0=arep[g][:].rearrange("n (w e) -> n e w", e=2),
+                scalar=gain[:, 0:1],
+                in1=ow[:, 512 * g : 512 * (g + 1)].rearrange("n (w e) -> n e w", e=2),
+                op0=MULT,
+                op1=ADD,
+            )
+
+        w_grp = consts.tile([P, 2, P, 4], BF16, name="w_grp", align_bytes=64)
+        w_codes = consts.tile([P, 2 * P], U32, name="w_codes", align_bytes=64)
+        w_scl = consts.tile([P, 2 * P], U8, name="w_scl", align_bytes=64)
+
+        def w_transposes():
+            for g in (1, 0):
+                wt = psum.tile([P, 4, P], BF16, tag="acc%d" % g, name="wt%d" % g)
+                for u in range(2):
+                    for e in range(2):
+                        nc.tensor.transpose(
+                            wt[:, 2 * u + e, :], w_d[:, e, g, P * u : P * (u + 1)], ident_b[:]
+                        )
+                nc.vector.tensor_copy(out=w_grp[:, g], in_=wt[:].rearrange("p t n -> p n t"))
+
+        def w_quantise():
+            nc.vector.quantize_mx(
+                out=w_codes[:].bitcast(FP8X4),
+                scales=w_scl[:],
+                in_=w_grp[:].rearrange("p g n t -> p (g n t)"),
+            )
+
+        banks = {}
+        grps = {}
+        quants = {}
+        accs = {}
+
+        def transposes(r):
+            tiles = []
+            for j in range(ROUND):
+                i = ROUND * r + j
+                xt = psum.tile([P, 4, P], F32, tag="xt%d" % (i % XT_BANKS), name="xt")
+                src, col = x_words[i]
+                for q in range(4):
+                    nc.tensor.transpose(
+                        xt[:, q, :], src[:, col + P * q : col + P * (q + 1)], ident_f[:]
+                    )
+                tiles.append(xt)
+            banks[r] = tiles
+
+        def copies(r):
+            grp = work.tile([P, ROUND * K], BF16, tag="grp", name="grp", align_bytes=64)
+            grp_w = grp[:].bitcast(F32).rearrange(
+                "p (j g m u) -> p j g m u", j=ROUND, g=2, m=P, u=2
+            )
+            for j in range(ROUND):
+                src = banks[r][j][:].rearrange("p (g u) m -> p g m u", u=2)
+                if j == 0:
+                    nc.vector.tensor_copy(out=grp_w[:, j], in_=src)
+                else:
+                    nc.scalar.copy(out=grp_w[:, j], in_=src)
+            grps[r] = grp
+
+        def quantise(r):
+            codes = work.tile([P, ROUND * 2 * P], U32, tag="codes", name="codes", align_bytes=64)
+            scl = work.tile([P, ROUND * 2 * P], U8, tag="scl", name="scl", align_bytes=64)
+            nc.vector.quantize_mx(out=codes[:].bitcast(FP8X4), scales=scl[:], in_=grps[r][:])
+            quants[r] = (codes, scl)
+
+        def products(r):
+            codes, scl = quants[r]
+            acc = psum.tile([P, ROUND * N_OUT], F32, tag="acc%d" % (r % 2), name="acc")
+            for j in range(ROUND):
+                for g in range(2):
+                    cols = slice((2 * j + g) * P, (2 * j + g + 1) * P)
+                    nc.tensor.matmul_mx(
+                        out=acc[:, j * N_OUT : (j + 1) * N_OUT],
+                        lhsT=codes[:, cols].bitcast(FP8X4),
+                        lhsT_scale=scl[:, cols],
+                        rhs=w_codes[:, g * P : (g + 1) * P].bitcast(FP8X4),
+                        rhs_scale=w_scl[:, g * P : (g + 1) * P],
+                        start=(g == 0),
+                        stop=(g == 1),
+                    )
+            accs[r] = acc
+
+        out_tiles = []
+        first = 0
+        for s, width in enumerate(STORE_GROUPS):
+            ot = opool.tile([P, width * N_OUT], F32, name="o%d" % s)
+            out_tiles.append((ot, first, width))
+            first += width
+
+        def results(r):
+            tile0 = ROUND * r
+            for ot, first_tile, width in out_tiles:
+                if first_tile <= tile0 < first_tile + width:
+                    off = (tile0 - first_tile) * N_OUT
+                    dst = ot[:, off : off + ROUND * N_OUT]
+                    if r % 2 == 0:
+                        nc.scalar.copy(out=dst, in_=accs[r][:])
+                    else:
+                        nc.vector.tensor_copy(out=dst, in_=accs[r][:])
+                    if tile0 + ROUND == first_tile + width:
+                        nc.sync.dma_start(
+                            out=out_v[:, first_tile : first_tile + width, :].rearrange(
+                                "p t n -> p (t n)"
+                            ),
+                            in_=ot[:],
+                        )
+
+        for s in range(N_ROUNDS + 3):
+            if s < N_ROUNDS:
+                transposes(s)
+            if 0 <= s - 3 < N_ROUNDS:
+                results(s - 3)
+            if s < N_ROUNDS:
+                copies(s)
+            if s == 0:
+                w_transposes()
+            if s == 1:
+                w_quantise()
+            if 0 <= s - 1 < N_ROUNDS:
+                quantise(s - 1)
+            if 0 <= s - 2 < N_ROUNDS:
+                products(s - 2)

@@ -17,10 +17,12 @@ M_ROWS = 8192
 K = 1024
 N_OUT = 128
 N_TILES = M_ROWS // P
-ROUND = 4
-N_ROUNDS = N_TILES // ROUND
+UNIT = 4
+GROUP = 8
+N_GROUPS = N_TILES // GROUP
 XT_BANKS = 6
-LOAD_CHUNKS = [1, 1, 2, 4, 8, 8, 8, 8, 8, 8, 4, 4]
+VECTOR_TILES = (2, 5)
+LOAD_CHUNKS = [1, 1, 2] + [4] * 15
 STORE_GROUPS = [16, 16, 16, 8, 4, 4]
 SCALING = 2.0
 
@@ -36,7 +38,8 @@ def tile_lokrlayer_t_kernel(tc, x, original_weight, lokr_A, lokr_B, scalar, out)
         consts = ctx.enter_context(tc.tile_pool(name="consts", bufs=1))
         xpool = ctx.enter_context(tc.tile_pool(name="xpool", bufs=1))
         opool = ctx.enter_context(tc.tile_pool(name="opool", bufs=1))
-        work = ctx.enter_context(tc.tile_pool(name="work", bufs=3))
+        gpool = ctx.enter_context(tc.tile_pool(name="gpool", bufs=3))
+        qpool = ctx.enter_context(tc.tile_pool(name="qpool", bufs=4))
         psum = ctx.enter_context(tc.psum_pool(name="psum", bufs=1))
         ctx.enter_context(tc.manual_schedule())
 
@@ -87,35 +90,38 @@ def tile_lokrlayer_t_kernel(tc, x, original_weight, lokr_A, lokr_B, scalar, out)
         nc.vector.tensor_copy(out=ident_b[:], in_=ident_f[:])
         sel2 = sel[:].rearrange("p a b -> p (a b)")
 
-        small = psum.tile([P, 512], F32, tag="acc0", name="small")
-        nc.tensor.matmul(small[:, 0:64], lhsT=sel2, rhs=par[:, K : K + 64], start=True, stop=True)
-        arep1 = psum.tile([P, 512], F32, tag="acc1", name="arep1")
-        nc.tensor.matmul(arep1[:], lhsT=sel2, rhs=par[:, 512:1024], start=True, stop=True)
-        cs = consts.tile([P, 2], F32, name="cs")
-        nc.vector.tensor_copy(out=cs[:], in_=small[:, 0:2])
-        arep0 = psum.tile([P, 512], F32, tag="acc0", name="arep0")
-        nc.tensor.matmul(arep0[:], lhsT=sel2, rhs=par[:, 0:512], start=True, stop=True)
-        gain = consts.tile([P, 1], F32, name="gain")
-        nc.vector.tensor_scalar(
-            out=gain[:], in0=cs[:, 0:1], scalar1=cs[:, 1:2], scalar2=SCALING, op0=MULT, op1=MULT
-        )
         w_d = consts.tile([P, 2, 2, 256], BF16, name="w_d")
-        arep = [arep0, arep1]
-        for g in (1, 0):
-            nc.vector.scalar_tensor_tensor(
-                out=w_d[:, :, g, :],
-                in0=arep[g][:].rearrange("n (w e) -> n e w", e=2),
-                scalar=gain[:, 0:1],
-                in1=ow[:, 512 * g : 512 * (g + 1)].rearrange("n (w e) -> n e w", e=2),
-                op0=MULT,
-                op1=ADD,
-            )
-
         w_grp = consts.tile([P, 2, P, 4], BF16, name="w_grp", align_bytes=64)
         w_codes = consts.tile([P, 2 * P], U32, name="w_codes", align_bytes=64)
         w_scl = consts.tile([P, 2 * P], U8, name="w_scl", align_bytes=64)
 
-        def w_transposes():
+        def w_form():
+            small = psum.tile([P, 512], F32, tag="acc0", name="small")
+            nc.tensor.matmul(
+                small[:, 0:64], lhsT=sel2, rhs=par[:, K : K + 64], start=True, stop=True
+            )
+            arep1 = psum.tile([P, 512], F32, tag="acc1", name="arep1")
+            nc.tensor.matmul(arep1[:], lhsT=sel2, rhs=par[:, 512:1024], start=True, stop=True)
+            cs = consts.tile([P, 2], F32, name="cs")
+            nc.vector.tensor_copy(out=cs[:], in_=small[:, 0:2])
+            arep0 = psum.tile([P, 512], F32, tag="acc0", name="arep0")
+            nc.tensor.matmul(arep0[:], lhsT=sel2, rhs=par[:, 0:512], start=True, stop=True)
+            gain = consts.tile([P, 1], F32, name="gain")
+            nc.vector.tensor_scalar(
+                out=gain[:], in0=cs[:, 0:1], scalar1=cs[:, 1:2], scalar2=SCALING, op0=MULT, op1=MULT
+            )
+            arep = [arep0, arep1]
+            for g in (1, 0):
+                nc.vector.scalar_tensor_tensor(
+                    out=w_d[:, :, g, :],
+                    in0=arep[g][:].rearrange("n (w e) -> n e w", e=2),
+                    scalar=gain[:, 0:1],
+                    in1=ow[:, 512 * g : 512 * (g + 1)].rearrange("n (w e) -> n e w", e=2),
+                    op0=MULT,
+                    op1=ADD,
+                )
+
+        def w_quantise():
             for g in (1, 0):
                 wt = psum.tile([P, 4, P], BF16, tag="acc%d" % g, name="wt%d" % g)
                 for u in range(2):
@@ -124,8 +130,6 @@ def tile_lokrlayer_t_kernel(tc, x, original_weight, lokr_A, lokr_B, scalar, out)
                             wt[:, 2 * u + e, :], w_d[:, e, g, P * u : P * (u + 1)], ident_b[:]
                         )
                 nc.vector.tensor_copy(out=w_grp[:, g], in_=wt[:].rearrange("p t n -> p n t"))
-
-        def w_quantise():
             nc.vector.quantize_mx(
                 out=w_codes[:].bitcast(FP8X4),
                 scales=w_scl[:],
@@ -137,42 +141,38 @@ def tile_lokrlayer_t_kernel(tc, x, original_weight, lokr_A, lokr_B, scalar, out)
         quants = {}
         accs = {}
 
-        def transposes(r):
-            tiles = []
-            for j in range(ROUND):
-                i = ROUND * r + j
-                xt = psum.tile([P, 4, P], F32, tag="xt%d" % (i % XT_BANKS), name="xt")
-                src, col = x_words[i]
-                for q in range(4):
-                    nc.tensor.transpose(
-                        xt[:, q, :], src[:, col + P * q : col + P * (q + 1)], ident_f[:]
-                    )
-                tiles.append(xt)
-            banks[r] = tiles
+        def transposes(i):
+            xt = psum.tile([P, 4, P], F32, tag="xt%d" % (i % XT_BANKS), name="xt")
+            src, col = x_words[i]
+            for q in range(4):
+                nc.tensor.transpose(
+                    xt[:, q, :], src[:, col + P * q : col + P * (q + 1)], ident_f[:]
+                )
+            banks[i] = xt
 
-        def copies(r):
-            grp = work.tile([P, ROUND * K], BF16, tag="grp", name="grp", align_bytes=64)
-            grp_w = grp[:].bitcast(F32).rearrange(
-                "p (j g m u) -> p j g m u", j=ROUND, g=2, m=P, u=2
-            )
-            for j in range(ROUND):
-                src = banks[r][j][:].rearrange("p (g u) m -> p g m u", u=2)
-                if j == 0:
-                    nc.vector.tensor_copy(out=grp_w[:, j], in_=src)
-                else:
-                    nc.scalar.copy(out=grp_w[:, j], in_=src)
-            grps[r] = grp
+        def copy_out(i, on_vector):
+            u, j = divmod(i, UNIT)
+            if j == 0:
+                grps[u] = gpool.tile([P, UNIT * K], BF16, tag="grp", name="grp", align_bytes=64)
+            dst = grps[u][:].bitcast(F32).rearrange(
+                "p (j g m u) -> p j g m u", j=UNIT, g=2, m=P, u=2
+            )[:, j]
+            src = banks[i][:].rearrange("p (g u) m -> p g m u", u=2)
+            if on_vector:
+                nc.vector.tensor_copy(out=dst, in_=src)
+            else:
+                nc.scalar.copy(out=dst, in_=src)
 
-        def quantise(r):
-            codes = work.tile([P, ROUND * 2 * P], U32, tag="codes", name="codes", align_bytes=64)
-            scl = work.tile([P, ROUND * 2 * P], U8, tag="scl", name="scl", align_bytes=64)
-            nc.vector.quantize_mx(out=codes[:].bitcast(FP8X4), scales=scl[:], in_=grps[r][:])
-            quants[r] = (codes, scl)
+        def quantise(u):
+            codes = qpool.tile([P, UNIT * 2 * P], U32, tag="codes", name="codes", align_bytes=64)
+            scl = qpool.tile([P, UNIT * 2 * P], U8, tag="scl", name="scl", align_bytes=64)
+            nc.vector.quantize_mx(out=codes[:].bitcast(FP8X4), scales=scl[:], in_=grps[u][:])
+            quants[u] = (codes, scl)
 
-        def products(r):
-            codes, scl = quants[r]
-            acc = psum.tile([P, ROUND * N_OUT], F32, tag="acc%d" % (r % 2), name="acc")
-            for j in range(ROUND):
+        def products(u):
+            codes, scl = quants[u]
+            acc = psum.tile([P, UNIT * N_OUT], F32, tag="acc%d" % (u % 2), name="acc")
+            for j in range(UNIT):
                 for g in range(2):
                     cols = slice((2 * j + g) * P, (2 * j + g + 1) * P)
                     nc.tensor.matmul_mx(
@@ -184,7 +184,7 @@ def tile_lokrlayer_t_kernel(tc, x, original_weight, lokr_A, lokr_B, scalar, out)
                         start=(g == 0),
                         stop=(g == 1),
                     )
-            accs[r] = acc
+            accs[u] = acc
 
         out_tiles = []
         first = 0
@@ -193,17 +193,17 @@ def tile_lokrlayer_t_kernel(tc, x, original_weight, lokr_A, lokr_B, scalar, out)
             out_tiles.append((ot, first, width))
             first += width
 
-        def results(r):
-            tile0 = ROUND * r
+        def results(u, on_vector):
+            tile0 = UNIT * u
             for ot, first_tile, width in out_tiles:
                 if first_tile <= tile0 < first_tile + width:
                     off = (tile0 - first_tile) * N_OUT
-                    dst = ot[:, off : off + ROUND * N_OUT]
-                    if r % 2 == 0:
-                        nc.scalar.copy(out=dst, in_=accs[r][:])
+                    dst = ot[:, off : off + UNIT * N_OUT]
+                    if on_vector:
+                        nc.vector.tensor_copy(out=dst, in_=accs[u][:])
                     else:
-                        nc.vector.tensor_copy(out=dst, in_=accs[r][:])
-                    if tile0 + ROUND == first_tile + width:
+                        nc.scalar.copy(out=dst, in_=accs[u][:])
+                    if tile0 + UNIT == first_tile + width:
                         nc.sync.dma_start(
                             out=out_v[:, first_tile : first_tile + width, :].rearrange(
                                 "p t n -> p (t n)"
@@ -211,18 +211,30 @@ def tile_lokrlayer_t_kernel(tc, x, original_weight, lokr_A, lokr_B, scalar, out)
                             in_=ot[:],
                         )
 
-        for s in range(N_ROUNDS + 3):
-            if s < N_ROUNDS:
-                transposes(s)
-            if 0 <= s - 3 < N_ROUNDS:
-                results(s - 3)
-            if s < N_ROUNDS:
-                copies(s)
+        for s in range(N_GROUPS + 2):
+            streaming = s < N_GROUPS
+            if streaming:
+                for j in range(XT_BANKS):
+                    transposes(GROUP * s + j)
+                    if s == 0 and j == UNIT - 1:
+                        w_form()
+            if 1 <= s <= N_GROUPS:
+                quantise(2 * s - 1)
+            if s >= 2:
+                results(2 * s - 4, False)
+            if streaming:
+                for j in range(GROUP):
+                    copy_out(GROUP * s + j, j in VECTOR_TILES)
+                    if j + XT_BANKS < GROUP:
+                        transposes(GROUP * s + j + XT_BANKS)
+                    if j == VECTOR_TILES[0] and s >= 2:
+                        results(2 * s - 3, True)
+            elif s >= 2:
+                results(2 * s - 3, True)
             if s == 0:
-                w_transposes()
-            if s == 1:
                 w_quantise()
-            if 0 <= s - 1 < N_ROUNDS:
-                quantise(s - 1)
-            if 0 <= s - 2 < N_ROUNDS:
-                products(s - 2)
+            if streaming:
+                quantise(2 * s)
+            if 1 <= s <= N_GROUPS:
+                products(2 * s - 2)
+                products(2 * s - 1)

@@ -22,8 +22,8 @@ GROUP = 8
 N_GROUPS = N_TILES // GROUP
 XT_BANKS = 6
 VECTOR_TILES = (2, 5)
-LOAD_CHUNKS = [1, 1, 2] + [4] * 15
-STORE_GROUPS = [16, 16, 16, 8, 4, 4]
+LOAD_CHUNKS = [4, 4, 8, 8, 8, 8, 8, 8, 4, 4]
+STORE_GROUPS = [32, 16, 8, 4, 4]
 SCALING = 2.0
 
 FLOPS = 2 * M_ROWS * K * N_OUT
@@ -69,10 +69,10 @@ def tile_lokrlayer_t_kernel(tc, x, original_weight, lokr_A, lokr_B, scalar, out)
             load(c)
 
         ow = consts.tile([P, K], BF16, name="ow")
+        nc.scalar.dma_start(out=ow[:], in_=original_weight)
         nc.scalar.dma_start(out=par[0:8, 0:K], in_=lokr_A)
         nc.scalar.dma_start(out=par[8:24, K : K + 1], in_=lokr_B)
         nc.scalar.dma_start(out=par[24:25, K + 1 : K + 2], in_=scalar.unsqueeze(0))
-        nc.scalar.dma_start(out=ow[:], in_=original_weight)
 
         for c in range(4, len(LOAD_CHUNKS)):
             load(c)
@@ -230,7 +230,7 @@ def tile_lokrlayer_t_kernel(tc, x, original_weight, lokr_A, lokr_B, scalar, out)
                     if j == VECTOR_TILES[0] and s >= 2:
                         results(2 * s - 3, True)
             elif s >= 2:
-                results(2 * s - 3, True)
+                results(2 * s - 3, s > N_GROUPS)
             if s == 0:
                 w_quantise()
             if streaming:

@@ -17,13 +17,13 @@ M_ROWS = 8192
 K = 1024
 N_OUT = 128
 N_TILES = M_ROWS // P
-UNIT = 4
 GROUP = 8
 N_GROUPS = N_TILES // GROUP
+UNIT_SIZES = [4] * 15 + [2, 2]
 XT_BANKS = 6
 VECTOR_TILES = (2, 5)
-LOAD_CHUNKS = [4, 4, 8, 8, 8, 8, 8, 8, 4, 4]
-STORE_GROUPS = [32, 16, 8, 4, 4]
+LOAD_CHUNKS = [2, 2] + [4] * 15
+STORE_GROUPS = [16, 16, 16, 8, 4, 4]
 SCALING = 2.0
 
 FLOPS = 2 * M_ROWS * K * N_OUT
@@ -33,6 +33,15 @@ def tile_lokrlayer_t_kernel(tc, x, original_weight, lokr_A, lokr_B, scalar, out)
     nc = tc.nc
     x_v = x.rearrange("(p t) k -> p t k", t=N_TILES)
     out_v = out.rearrange("(p t) n -> p t n", t=N_TILES)
+
+    unit_first = [sum(UNIT_SIZES[:u]) for u in range(len(UNIT_SIZES))]
+    unit_of = {}
+    for u, size in enumerate(UNIT_SIZES):
+        for j in range(size):
+            unit_of[unit_first[u] + j] = u
+    group_units = [
+        [u for u in range(len(UNIT_SIZES)) if unit_first[u] // GROUP == g] for g in range(N_GROUPS)
+    ]
 
     with ExitStack() as ctx:
         consts = ctx.enter_context(tc.tile_pool(name="consts", bufs=1))
@@ -151,11 +160,13 @@ def tile_lokrlayer_t_kernel(tc, x, original_weight, lokr_A, lokr_B, scalar, out)
             banks[i] = xt
 
         def copy_out(i, on_vector):
-            u, j = divmod(i, UNIT)
+            u = unit_of[i]
+            j = i - unit_first[u]
+            size = UNIT_SIZES[u]
             if j == 0:
-                grps[u] = gpool.tile([P, UNIT * K], BF16, tag="grp", name="grp", align_bytes=64)
+                grps[u] = gpool.tile([P, size * K], BF16, tag="grp", name="grp", align_bytes=64)
             dst = grps[u][:].bitcast(F32).rearrange(
-                "p (j g m u) -> p j g m u", j=UNIT, g=2, m=P, u=2
+                "p (j g m u) -> p j g m u", j=size, g=2, m=P, u=2
             )[:, j]
             src = banks[i][:].rearrange("p (g u) m -> p g m u", u=2)
             if on_vector:
@@ -164,15 +175,18 @@ def tile_lokrlayer_t_kernel(tc, x, original_weight, lokr_A, lokr_B, scalar, out)
                 nc.scalar.copy(out=dst, in_=src)
 
         def quantise(u):
-            codes = qpool.tile([P, UNIT * 2 * P], U32, tag="codes", name="codes", align_bytes=64)
-            scl = qpool.tile([P, UNIT * 2 * P], U8, tag="scl", name="scl", align_bytes=64)
+            size = UNIT_SIZES[u]
+            codes = qpool.tile([P, size * 2 * P], U32, tag="codes", name="codes", align_bytes=64)
+            scl = qpool.tile([P, size * 2 * P], U8, tag="scl", name="scl", align_bytes=64)
             nc.vector.quantize_mx(out=codes[:].bitcast(FP8X4), scales=scl[:], in_=grps[u][:])
             quants[u] = (codes, scl)
 
         def products(u):
             codes, scl = quants[u]
-            acc = psum.tile([P, UNIT * N_OUT], F32, tag="acc%d" % (u % 2), name="acc")
-            for j in range(UNIT):
+            size = UNIT_SIZES[u]
+            tag = "acc%d" % (u % 2) if u < 16 else "xt0"
+            acc = psum.tile([P, size * N_OUT], F32, tag=tag, name="acc")
+            for j in range(size):
                 for g in range(2):
                     cols = slice((2 * j + g) * P, (2 * j + g + 1) * P)
                     nc.tensor.matmul_mx(
@@ -194,16 +208,17 @@ def tile_lokrlayer_t_kernel(tc, x, original_weight, lokr_A, lokr_B, scalar, out)
             first += width
 
         def results(u, on_vector):
-            tile0 = UNIT * u
+            tile0 = unit_first[u]
+            size = UNIT_SIZES[u]
             for ot, first_tile, width in out_tiles:
                 if first_tile <= tile0 < first_tile + width:
                     off = (tile0 - first_tile) * N_OUT
-                    dst = ot[:, off : off + UNIT * N_OUT]
+                    dst = ot[:, off : off + size * N_OUT]
                     if on_vector:
                         nc.vector.tensor_copy(out=dst, in_=accs[u][:])
                     else:
                         nc.scalar.copy(out=dst, in_=accs[u][:])
-                    if tile0 + UNIT == first_tile + width:
+                    if tile0 + size == first_tile + width:
                         nc.sync.dma_start(
                             out=out_v[:, first_tile : first_tile + width, :].rearrange(
                                 "p t n -> p (t n)"
@@ -213,28 +228,35 @@ def tile_lokrlayer_t_kernel(tc, x, original_weight, lokr_A, lokr_B, scalar, out)
 
         for s in range(N_GROUPS + 2):
             streaming = s < N_GROUPS
+            mine = group_units[s] if streaming else []
+            before = group_units[s - 1] if 1 <= s <= N_GROUPS else []
+            older = group_units[s - 2] if s >= 2 else []
             if streaming:
                 for j in range(XT_BANKS):
                     transposes(GROUP * s + j)
-                    if s == 0 and j == UNIT - 1:
-                        w_form()
-            if 1 <= s <= N_GROUPS:
-                quantise(2 * s - 1)
-            if s >= 2:
-                results(2 * s - 4, False)
+            if before:
+                quantise(before[-1])
+            if older:
+                results(older[0], False)
             if streaming:
                 for j in range(GROUP):
+                    if j == VECTOR_TILES[1]:
+                        quantise(mine[0])
                     copy_out(GROUP * s + j, j in VECTOR_TILES)
                     if j + XT_BANKS < GROUP:
                         transposes(GROUP * s + j + XT_BANKS)
-                    if j == VECTOR_TILES[0] and s >= 2:
-                        results(2 * s - 3, True)
-            elif s >= 2:
-                results(2 * s - 3, s > N_GROUPS)
+                    if j == VECTOR_TILES[0] and older:
+                        results(older[1], True)
+                    if j == VECTOR_TILES[1]:
+                        for u in mine[1:-1]:
+                            quantise(u)
+            elif s == N_GROUPS:
+                results(older[1], False)
+            else:
+                results(older[1], True)
+                results(older[2], False)
             if s == 0:
+                w_form()
                 w_quantise()
-            if streaming:
-                quantise(2 * s)
-            if 1 <= s <= N_GROUPS:
-                products(2 * s - 2)
-                products(2 * s - 1)
+            for u in before:
+                products(u)

@@ -17,12 +17,10 @@ M_ROWS = 8192
 K = 1024
 N_OUT = 128
 N_TILES = M_ROWS // P
-GROUP = 8
-N_GROUPS = N_TILES // GROUP
-UNIT_SIZES = [4] * 15 + [2, 2]
+ROUND = 4
+N_ROUNDS = N_TILES // ROUND
 XT_BANKS = 6
-VECTOR_TILES = (2, 5)
-LOAD_CHUNKS = [2, 2] + [4] * 15
+LOAD_CHUNKS = [1, 1, 2] + [4] * 15
 STORE_GROUPS = [16, 16, 16, 8, 4, 4]
 SCALING = 2.0
 
@@ -34,21 +32,11 @@ def tile_lokrlayer_t_kernel(tc, x, original_weight, lokr_A, lokr_B, scalar, out)
     x_v = x.rearrange("(p t) k -> p t k", t=N_TILES)
     out_v = out.rearrange("(p t) n -> p t n", t=N_TILES)
 
-    unit_first = [sum(UNIT_SIZES[:u]) for u in range(len(UNIT_SIZES))]
-    unit_of = {}
-    for u, size in enumerate(UNIT_SIZES):
-        for j in range(size):
-            unit_of[unit_first[u] + j] = u
-    group_units = [
-        [u for u in range(len(UNIT_SIZES)) if unit_first[u] // GROUP == g] for g in range(N_GROUPS)
-    ]
-
     with ExitStack() as ctx:
         consts = ctx.enter_context(tc.tile_pool(name="consts", bufs=1))
         xpool = ctx.enter_context(tc.tile_pool(name="xpool", bufs=1))
         opool = ctx.enter_context(tc.tile_pool(name="opool", bufs=1))
-        gpool = ctx.enter_context(tc.tile_pool(name="gpool", bufs=3))
-        qpool = ctx.enter_context(tc.tile_pool(name="qpool", bufs=4))
+        work = ctx.enter_context(tc.tile_pool(name="work", bufs=3))
         psum = ctx.enter_context(tc.psum_pool(name="psum", bufs=1))
         ctx.enter_context(tc.manual_schedule())
 
@@ -105,22 +93,24 @@ def tile_lokrlayer_t_kernel(tc, x, original_weight, lokr_A, lokr_B, scalar, out)
         w_scl = consts.tile([P, 2 * P], U8, name="w_scl", align_bytes=64)
 
         def w_form():
-            small = psum.tile([P, 512], F32, tag="acc0", name="small")
+            small = psum.tile([P, 512], F32, tag="xt5", name="small")
             nc.tensor.matmul(
                 small[:, 0:64], lhsT=sel2, rhs=par[:, K : K + 64], start=True, stop=True
             )
-            arep1 = psum.tile([P, 512], F32, tag="acc1", name="arep1")
-            nc.tensor.matmul(arep1[:], lhsT=sel2, rhs=par[:, 512:1024], start=True, stop=True)
+            arep = []
+            for g in range(2):
+                ps = psum.tile([P, 512], F32, tag="acc%d" % g, name="arep%d" % g)
+                nc.tensor.matmul(
+                    ps[:], lhsT=sel2, rhs=par[:, 512 * g : 512 * (g + 1)], start=True, stop=True
+                )
+                arep.append(ps)
             cs = consts.tile([P, 2], F32, name="cs")
             nc.vector.tensor_copy(out=cs[:], in_=small[:, 0:2])
-            arep0 = psum.tile([P, 512], F32, tag="acc0", name="arep0")
-            nc.tensor.matmul(arep0[:], lhsT=sel2, rhs=par[:, 0:512], start=True, stop=True)
             gain = consts.tile([P, 1], F32, name="gain")
             nc.vector.tensor_scalar(
                 out=gain[:], in0=cs[:, 0:1], scalar1=cs[:, 1:2], scalar2=SCALING, op0=MULT, op1=MULT
             )
-            arep = [arep0, arep1]
-            for g in (1, 0):
+            for g in range(2):
                 nc.vector.scalar_tensor_tensor(
                     out=w_d[:, :, g, :],
                     in0=arep[g][:].rearrange("n (w e) -> n e w", e=2),
@@ -131,7 +121,7 @@ def tile_lokrlayer_t_kernel(tc, x, original_weight, lokr_A, lokr_B, scalar, out)
                 )
 
         def w_quantise():
-            for g in (1, 0):
+            for g in range(2):
                 wt = psum.tile([P, 4, P], BF16, tag="acc%d" % g, name="wt%d" % g)
                 for u in range(2):
                     for e in range(2):
@@ -150,43 +140,42 @@ def tile_lokrlayer_t_kernel(tc, x, original_weight, lokr_A, lokr_B, scalar, out)
         quants = {}
         accs = {}
 
-        def transposes(i):
-            xt = psum.tile([P, 4, P], F32, tag="xt%d" % (i % XT_BANKS), name="xt")
-            src, col = x_words[i]
-            for q in range(4):
-                nc.tensor.transpose(
-                    xt[:, q, :], src[:, col + P * q : col + P * (q + 1)], ident_f[:]
-                )
-            banks[i] = xt
+        def transposes(r):
+            tiles = []
+            for j in range(ROUND):
+                i = ROUND * r + j
+                xt = psum.tile([P, 4, P], F32, tag="xt%d" % (i % XT_BANKS), name="xt")
+                src, col = x_words[i]
+                for q in range(4):
+                    nc.tensor.transpose(
+                        xt[:, q, :], src[:, col + P * q : col + P * (q + 1)], ident_f[:]
+                    )
+                tiles.append(xt)
+            banks[r] = tiles
 
-        def copy_out(i, on_vector):
-            u = unit_of[i]
-            j = i - unit_first[u]
-            size = UNIT_SIZES[u]
-            if j == 0:
-                grps[u] = gpool.tile([P, size * K], BF16, tag="grp", name="grp", align_bytes=64)
-            dst = grps[u][:].bitcast(F32).rearrange(
-                "p (j g m u) -> p j g m u", j=size, g=2, m=P, u=2
-            )[:, j]
-            src = banks[i][:].rearrange("p (g u) m -> p g m u", u=2)
-            if on_vector:
-                nc.vector.tensor_copy(out=dst, in_=src)
-            else:
-                nc.scalar.copy(out=dst, in_=src)
+        def copies(r):
+            grp = work.tile([P, ROUND * K], BF16, tag="grp", name="grp", align_bytes=64)
+            grp_w = grp[:].bitcast(F32).rearrange(
+                "p (j g m u) -> p j g m u", j=ROUND, g=2, m=P, u=2
+            )
+            for j in range(ROUND):
+                src = banks[r][j][:].rearrange("p (g u) m -> p g m u", u=2)
+                if j == 0:
+                    nc.vector.tensor_copy(out=grp_w[:, j], in_=src)
+                else:
+                    nc.scalar.copy(out=grp_w[:, j], in_=src)
+            grps[r] = grp
 
-        def quantise(u):
-            size = UNIT_SIZES[u]
-            codes = qpool.tile([P, size * 2 * P], U32, tag="codes", name="codes", align_bytes=64)
-            scl = qpool.tile([P, size * 2 * P], U8, tag="scl", name="scl", align_bytes=64)
-            nc.vector.quantize_mx(out=codes[:].bitcast(FP8X4), scales=scl[:], in_=grps[u][:])
-            quants[u] = (codes, scl)
+        def quantise(r):
+            codes = work.tile([P, ROUND * 2 * P], U32, tag="codes", name="codes", align_bytes=64)
+            scl = work.tile([P, ROUND * 2 * P], U8, tag="scl", name="scl", align_bytes=64)
+            nc.vector.quantize_mx(out=codes[:].bitcast(FP8X4), scales=scl[:], in_=grps[r][:])
+            quants[r] = (codes, scl)
 
-        def products(u):
-            codes, scl = quants[u]
-            size = UNIT_SIZES[u]
-            tag = "acc%d" % (u % 2) if u < 16 else "xt0"
-            acc = psum.tile([P, size * N_OUT], F32, tag=tag, name="acc")
-            for j in range(size):
+        def products(r):
+            codes, scl = quants[r]
+            acc = psum.tile([P, ROUND * N_OUT], F32, tag="acc%d" % (r % 2), name="acc")
+            for j in range(ROUND):
                 for g in range(2):
                     cols = slice((2 * j + g) * P, (2 * j + g + 1) * P)
                     nc.tensor.matmul_mx(
@@ -198,7 +187,7 @@ def tile_lokrlayer_t_kernel(tc, x, original_weight, lokr_A, lokr_B, scalar, out)
                         start=(g == 0),
                         stop=(g == 1),
                     )
-            accs[u] = acc
+            accs[r] = acc
 
         out_tiles = []
         first = 0
@@ -207,18 +196,17 @@ def tile_lokrlayer_t_kernel(tc, x, original_weight, lokr_A, lokr_B, scalar, out)
             out_tiles.append((ot, first, width))
             first += width
 
-        def results(u, on_vector):
-            tile0 = unit_first[u]
-            size = UNIT_SIZES[u]
+        def results(r):
+            tile0 = ROUND * r
             for ot, first_tile, width in out_tiles:
                 if first_tile <= tile0 < first_tile + width:
                     off = (tile0 - first_tile) * N_OUT
-                    dst = ot[:, off : off + size * N_OUT]
-                    if on_vector:
-                        nc.vector.tensor_copy(out=dst, in_=accs[u][:])
+                    dst = ot[:, off : off + ROUND * N_OUT]
+                    if r % 2 == 1 and r != N_ROUNDS - 3:
+                        nc.vector.tensor_copy(out=dst, in_=accs[r][:])
                     else:
-                        nc.scalar.copy(out=dst, in_=accs[u][:])
-                    if tile0 + size == first_tile + width:
+                        nc.scalar.copy(out=dst, in_=accs[r][:])
+                    if tile0 + ROUND == first_tile + width:
                         nc.sync.dma_start(
                             out=out_v[:, first_tile : first_tile + width, :].rearrange(
                                 "p t n -> p (t n)"
@@ -226,37 +214,18 @@ def tile_lokrlayer_t_kernel(tc, x, original_weight, lokr_A, lokr_B, scalar, out)
                             in_=ot[:],
                         )
 
-        for s in range(N_GROUPS + 2):
-            streaming = s < N_GROUPS
-            mine = group_units[s] if streaming else []
-            before = group_units[s - 1] if 1 <= s <= N_GROUPS else []
-            older = group_units[s - 2] if s >= 2 else []
-            if streaming:
-                for j in range(XT_BANKS):
-                    transposes(GROUP * s + j)
-            if before:
-                quantise(before[-1])
-            if older:
-                results(older[0], False)
-            if streaming:
-                for j in range(GROUP):
-                    if j == VECTOR_TILES[1]:
-                        quantise(mine[0])
-                    copy_out(GROUP * s + j, j in VECTOR_TILES)
-                    if j + XT_BANKS < GROUP:
-                        transposes(GROUP * s + j + XT_BANKS)
-                    if j == VECTOR_TILES[0] and older:
-                        results(older[1], True)
-                    if j == VECTOR_TILES[1]:
-                        for u in mine[1:-1]:
-                            quantise(u)
-            elif s == N_GROUPS:
-                results(older[1], False)
-            else:
-                results(older[1], True)
-                results(older[2], False)
+        for s in range(N_ROUNDS + 3):
+            if s < N_ROUNDS:
+                transposes(s)
+            if 0 <= s - 3 < N_ROUNDS:
+                results(s - 3)
+            if s < N_ROUNDS:
+                copies(s)
             if s == 0:
                 w_form()
+            if s == 1:
                 w_quantise()
-            for u in before:
-                products(u)
+            if 0 <= s - 1 < N_ROUNDS:
+                quantise(s - 1)
+            if 0 <= s - 2 < N_ROUNDS:
+                products(s - 2)

@@ -17,9 +17,12 @@ M_ROWS = 8192
 K = 1024
 N_OUT = 128
 N_TILES = M_ROWS // P
-ROUND = 4
-N_ROUNDS = N_TILES // ROUND
+UNIT = 4
+GROUP = 8
+N_GROUPS = N_TILES // GROUP
+SUPER = 16
 XT_BANKS = 6
+VECTOR_TILES = (2, 5)
 LOAD_CHUNKS = [1, 1, 2] + [4] * 15
 STORE_GROUPS = [16, 16, 16, 8, 4, 4]
 SCALING = 2.0
@@ -29,14 +32,15 @@ FLOPS = 2 * M_ROWS * K * N_OUT
 
 def tile_lokrlayer_t_kernel(tc, x, original_weight, lokr_A, lokr_B, scalar, out):
     nc = tc.nc
-    x_v = x.rearrange("(p t) k -> p t k", t=N_TILES)
-    out_v = out.rearrange("(p t) n -> p t n", t=N_TILES)
+    x_v = x.rearrange("(c p t) k -> p c t k", p=P, t=SUPER)
+    out_v = out.rearrange("(c p t) n -> p c t n", p=P, t=SUPER)
 
     with ExitStack() as ctx:
         consts = ctx.enter_context(tc.tile_pool(name="consts", bufs=1))
         xpool = ctx.enter_context(tc.tile_pool(name="xpool", bufs=1))
         opool = ctx.enter_context(tc.tile_pool(name="opool", bufs=1))
-        work = ctx.enter_context(tc.tile_pool(name="work", bufs=3))
+        gpool = ctx.enter_context(tc.tile_pool(name="gpool", bufs=3))
+        qpool = ctx.enter_context(tc.tile_pool(name="qpool", bufs=4))
         psum = ctx.enter_context(tc.psum_pool(name="psum", bufs=1))
         ctx.enter_context(tc.manual_schedule())
 
@@ -58,18 +62,20 @@ def tile_lokrlayer_t_kernel(tc, x, original_weight, lokr_A, lokr_B, scalar, out)
 
         def load(c):
             xs, first, width = x_tiles[c]
+            c_sup, t_sup = divmod(first, SUPER)
             nc.sync.dma_start(
-                out=xs[:], in_=x_v[:, first : first + width, :].rearrange("p t k -> p (t k)")
+                out=xs[:],
+                in_=x_v[:, c_sup, t_sup : t_sup + width, :].rearrange("p t k -> p (t k)"),
             )
 
         for c in range(4):
             load(c)
 
         ow = consts.tile([P, K], BF16, name="ow")
-        nc.scalar.dma_start(out=ow[:], in_=original_weight)
         nc.scalar.dma_start(out=par[0:8, 0:K], in_=lokr_A)
         nc.scalar.dma_start(out=par[8:24, K : K + 1], in_=lokr_B)
         nc.scalar.dma_start(out=par[24:25, K + 1 : K + 2], in_=scalar.unsqueeze(0))
+        nc.scalar.dma_start(out=ow[:], in_=original_weight)
 
         for c in range(4, len(LOAD_CHUNKS)):
             load(c)
@@ -93,24 +99,22 @@ def tile_lokrlayer_t_kernel(tc, x, original_weight, lokr_A, lokr_B, scalar, out)
         w_scl = consts.tile([P, 2 * P], U8, name="w_scl", align_bytes=64)
 
         def w_form():
-            small = psum.tile([P, 512], F32, tag="xt5", name="small")
+            small = psum.tile([P, 512], F32, tag="acc0", name="small")
             nc.tensor.matmul(
                 small[:, 0:64], lhsT=sel2, rhs=par[:, K : K + 64], start=True, stop=True
             )
-            arep = []
-            for g in range(2):
-                ps = psum.tile([P, 512], F32, tag="acc%d" % g, name="arep%d" % g)
-                nc.tensor.matmul(
-                    ps[:], lhsT=sel2, rhs=par[:, 512 * g : 512 * (g + 1)], start=True, stop=True
-                )
-                arep.append(ps)
+            arep1 = psum.tile([P, 512], F32, tag="acc1", name="arep1")
+            nc.tensor.matmul(arep1[:], lhsT=sel2, rhs=par[:, 512:1024], start=True, stop=True)
             cs = consts.tile([P, 2], F32, name="cs")
             nc.vector.tensor_copy(out=cs[:], in_=small[:, 0:2])
+            arep0 = psum.tile([P, 512], F32, tag="acc0", name="arep0")
+            nc.tensor.matmul(arep0[:], lhsT=sel2, rhs=par[:, 0:512], start=True, stop=True)
             gain = consts.tile([P, 1], F32, name="gain")
             nc.vector.tensor_scalar(
                 out=gain[:], in0=cs[:, 0:1], scalar1=cs[:, 1:2], scalar2=SCALING, op0=MULT, op1=MULT
             )
-            for g in range(2):
+            arep = [arep0, arep1]
+            for g in (1, 0):
                 nc.vector.scalar_tensor_tensor(
                     out=w_d[:, :, g, :],
                     in0=arep[g][:].rearrange("n (w e) -> n e w", e=2),
@@ -121,7 +125,7 @@ def tile_lokrlayer_t_kernel(tc, x, original_weight, lokr_A, lokr_B, scalar, out)
                 )
 
         def w_quantise():
-            for g in range(2):
+            for g in (1, 0):
                 wt = psum.tile([P, 4, P], BF16, tag="acc%d" % g, name="wt%d" % g)
                 for u in range(2):
                     for e in range(2):
@@ -140,42 +144,38 @@ def tile_lokrlayer_t_kernel(tc, x, original_weight, lokr_A, lokr_B, scalar, out)
         quants = {}
         accs = {}
 
-        def transposes(r):
-            tiles = []
-            for j in range(ROUND):
-                i = ROUND * r + j
-                xt = psum.tile([P, 4, P], F32, tag="xt%d" % (i % XT_BANKS), name="xt")
-                src, col = x_words[i]
-                for q in range(4):
-                    nc.tensor.transpose(
-                        xt[:, q, :], src[:, col + P * q : col + P * (q + 1)], ident_f[:]
-                    )
-                tiles.append(xt)
-            banks[r] = tiles
+        def transposes(i):
+            xt = psum.tile([P, 4, P], F32, tag="xt%d" % (i % XT_BANKS), name="xt")
+            src, col = x_words[i]
+            for q in range(4):
+                nc.tensor.transpose(
+                    xt[:, q, :], src[:, col + P * q : col + P * (q + 1)], ident_f[:]
+                )
+            banks[i] = xt
 
-        def copies(r):
-            grp = work.tile([P, ROUND * K], BF16, tag="grp", name="grp", align_bytes=64)
-            grp_w = grp[:].bitcast(F32).rearrange(
-                "p (j g m u) -> p j g m u", j=ROUND, g=2, m=P, u=2
-            )
-            for j in range(ROUND):
-                src = banks[r][j][:].rearrange("p (g u) m -> p g m u", u=2)
-                if j == 0:
-                    nc.vector.tensor_copy(out=grp_w[:, j], in_=src)
-                else:
-                    nc.scalar.copy(out=grp_w[:, j], in_=src)
-            grps[r] = grp
+        def copy_out(i, on_vector):
+            u, j = divmod(i, UNIT)
+            if j == 0:
+                grps[u] = gpool.tile([P, UNIT * K], BF16, tag="grp", name="grp", align_bytes=64)
+            dst = grps[u][:].bitcast(F32).rearrange(
+                "p (j g m u) -> p j g m u", j=UNIT, g=2, m=P, u=2
+            )[:, j]
+            src = banks[i][:].rearrange("p (g u) m -> p g m u", u=2)
+            if on_vector:
+                nc.vector.tensor_copy(out=dst, in_=src)
+            else:
+                nc.scalar.copy(out=dst, in_=src)
 
-        def quantise(r):
-            codes = work.tile([P, ROUND * 2 * P], U32, tag="codes", name="codes", align_bytes=64)
-            scl = work.tile([P, ROUND * 2 * P], U8, tag="scl", name="scl", align_bytes=64)
-            nc.vector.quantize_mx(out=codes[:].bitcast(FP8X4), scales=scl[:], in_=grps[r][:])
-            quants[r] = (codes, scl)
+        def quantise(u):
+            codes = qpool.tile([P, UNIT * 2 * P], U32, tag="codes", name="codes", align_bytes=64)
+            scl = qpool.tile([P, UNIT * 2 * P], U8, tag="scl", name="scl", align_bytes=64)
+            nc.vector.quantize_mx(out=codes[:].bitcast(FP8X4), scales=scl[:], in_=grps[u][:])
+            quants[u] = (codes, scl)
 
-        def products(r):
-            codes, scl = quants[r]
-            acc = psum.tile([P, ROUND * N_OUT], F32, tag="acc%d" % (r % 2), name="acc")
-            for j in range(ROUND):
+        def products(u):
+            codes, scl = quants[u]
+            acc = psum.tile([P, UNIT * N_OUT], F32, tag="acc%d" % (u % 2), name="acc")
+            for j in range(UNIT):
                 for g in range(2):
                     cols = slice((2 * j + g) * P, (2 * j + g + 1) * P)
                     nc.tensor.matmul_mx(
@@ -187,7 +187,7 @@ def tile_lokrlayer_t_kernel(tc, x, original_weight, lokr_A, lokr_B, scalar, out)
                         start=(g == 0),
                         stop=(g == 1),
                     )
-            accs[r] = acc
+            accs[u] = acc
 
         out_tiles = []
         first = 0
@@ -196,36 +196,49 @@ def tile_lokrlayer_t_kernel(tc, x, original_weight, lokr_A, lokr_B, scalar, out)
             out_tiles.append((ot, first, width))
             first += width
 
-        def results(r):
-            tile0 = ROUND * r
+        def results(u, on_vector):
+            tile0 = UNIT * u
             for ot, first_tile, width in out_tiles:
                 if first_tile <= tile0 < first_tile + width:
                     off = (tile0 - first_tile) * N_OUT
-                    dst = ot[:, off : off + ROUND * N_OUT]
-                    if r % 2 == 1 and r != N_ROUNDS - 3:
-                        nc.vector.tensor_copy(out=dst, in_=accs[r][:])
+                    dst = ot[:, off : off + UNIT * N_OUT]
+                    if on_vector:
+                        nc.vector.tensor_copy(out=dst, in_=accs[u][:])
                     else:
-                        nc.scalar.copy(out=dst, in_=accs[r][:])
-                    if tile0 + ROUND == first_tile + width:
+                        nc.scalar.copy(out=dst, in_=accs[u][:])
+                    if tile0 + UNIT == first_tile + width:
+                        c_sup, t_sup = divmod(first_tile, SUPER)
                         nc.sync.dma_start(
-                            out=out_v[:, first_tile : first_tile + width, :].rearrange(
+                            out=out_v[:, c_sup, t_sup : t_sup + width, :].rearrange(
                                 "p t n -> p (t n)"
                             ),
                             in_=ot[:],
                         )
 
-        for s in range(N_ROUNDS + 3):
-            if s < N_ROUNDS:
-                transposes(s)
-            if 0 <= s - 3 < N_ROUNDS:
-                results(s - 3)
-            if s < N_ROUNDS:
-                copies(s)
+        for s in range(N_GROUPS + 2):
+            streaming = s < N_GROUPS
+            if streaming:
+                for j in range(XT_BANKS):
+                    transposes(GROUP * s + j)
+                    if s == 0 and j == UNIT - 1:
+                        w_form()
+            if 1 <= s <= N_GROUPS:
+                quantise(2 * s - 1)
+            if s >= 2:
+                results(2 * s - 4, False)
+            if streaming:
+                for j in range(GROUP):
+                    copy_out(GROUP * s + j, j in VECTOR_TILES)
+                    if j + XT_BANKS < GROUP:
+                        transposes(GROUP * s + j + XT_BANKS)
+                    if j == VECTOR_TILES[0] and s >= 2:
+                        results(2 * s - 3, True)
+            elif s >= 2:
+                results(2 * s - 3, True)
             if s == 0:
-                w_form()
-            if s == 1:
                 w_quantise()
-            if 0 <= s - 1 < N_ROUNDS:
-                quantise(s - 1)
-            if 0 <= s - 2 < N_ROUNDS:
-                products(s - 2)
+            if streaming:
+                quantise(2 * s)
+            if 1 <= s <= N_GROUPS:
+                products(2 * s - 2)
+                products(2 * s - 1)

from contextlib import ExitStack

import concourse.mybir as mybir
from concourse.masks import make_identity

F32 = mybir.dt.float32
BF16 = mybir.dt.bfloat16
U32 = mybir.dt.uint32
U8 = mybir.dt.uint8
I32 = mybir.dt.int32
FP8X4 = mybir.dt.float8_e4m3fn_x4
ADD = mybir.AluOpType.add
MULT = mybir.AluOpType.mult

P = 128
M_ROWS = 8192
K = 1024
N_OUT = 128
N_TILES = M_ROWS // P
UNIT = 4
GROUP = 8
N_GROUPS = N_TILES // GROUP
SUPER = 16
XT_BANKS = 6
VECTOR_TILES = (2, 5)
LOAD_CHUNKS = [1, 1, 2] + [4] * 15
STORE_GROUPS = [16, 16, 16, 8, 4, 4]
SCALING = 2.0

FLOPS = 2 * M_ROWS * K * N_OUT


def tile_lokrlayer_t_kernel(tc, x, original_weight, lokr_A, lokr_B, scalar, out):
    nc = tc.nc
    x_v = x.rearrange("(c p t) k -> p c t k", p=P, t=SUPER)
    out_v = out.rearrange("(c p t) n -> p c t n", p=P, t=SUPER)

    with ExitStack() as ctx:
        consts = ctx.enter_context(tc.tile_pool(name="consts", bufs=1))
        xpool = ctx.enter_context(tc.tile_pool(name="xpool", bufs=1))
        opool = ctx.enter_context(tc.tile_pool(name="opool", bufs=1))
        gpool = ctx.enter_context(tc.tile_pool(name="gpool", bufs=3))
        qpool = ctx.enter_context(tc.tile_pool(name="qpool", bufs=4))
        psum = ctx.enter_context(tc.psum_pool(name="psum", bufs=1))
        ctx.enter_context(tc.manual_schedule())

        par = consts.tile([P, K + 64], BF16, name="par")
        nc.vector.memset(par[:].bitcast(I32), 0)
        ident_f = consts.tile([P, P], F32, name="ident_f")
        make_identity(nc, ident_f[:])

        x_words = []
        x_tiles = []
        t0 = 0
        for c, width in enumerate(LOAD_CHUNKS):
            xs = xpool.tile([P, width * K], BF16, name="x%d" % c)
            x_tiles.append((xs, t0, width))
            xw = xs[:].bitcast(F32)
            for j in range(width):
                x_words.append((xw, j * (K // 2)))
            t0 += width

        def load(c):
            xs, first, width = x_tiles[c]
            c_sup, t_sup = divmod(first, SUPER)
            nc.sync.dma_start(
                out=xs[:],
                in_=x_v[:, c_sup, t_sup : t_sup + width, :].rearrange("p t k -> p (t k)"),
            )

        for c in range(4):
            load(c)

        ow = consts.tile([P, K], BF16, name="ow")
        nc.scalar.dma_start(out=par[0:8, 0:K], in_=lokr_A)
        nc.scalar.dma_start(out=par[8:24, K : K + 1], in_=lokr_B)
        nc.scalar.dma_start(out=par[24:25, K + 1 : K + 2], in_=scalar.unsqueeze(0))
        nc.scalar.dma_start(out=ow[:], in_=original_weight)

        for c in range(4, len(LOAD_CHUNKS)):
            load(c)

        sel = consts.tile([P, 8, 16], BF16, name="sel")
        nc.vector.scalar_tensor_tensor(
            out=sel[:],
            in0=ident_f[:, 0:8].unsqueeze(2).to_broadcast([P, 8, 16]),
            scalar=ident_f[:, 24:25],
            in1=ident_f[:, 8:24].unsqueeze(1).to_broadcast([P, 8, 16]),
            op0=ADD,
            op1=ADD,
        )
        ident_b = consts.tile([P, P], BF16, name="ident_b")
        nc.vector.tensor_copy(out=ident_b[:], in_=ident_f[:])
        sel2 = sel[:].rearrange("p a b -> p (a b)")

        w_d = consts.tile([P, 2, 2, 256], BF16, name="w_d")
        w_grp = consts.tile([P, 2, P, 4], BF16, name="w_grp", align_bytes=64)
        w_codes = consts.tile([P, 2 * P], U32, name="w_codes", align_bytes=64)
        w_scl = consts.tile([P, 2 * P], U8, name="w_scl", align_bytes=64)

        def w_form():
            small = psum.tile([P, 512], F32, tag="acc0", name="small")
            nc.tensor.matmul(
                small[:, 0:64], lhsT=sel2, rhs=par[:, K : K + 64], start=True, stop=True
            )
            arep1 = psum.tile([P, 512], F32, tag="acc1", name="arep1")
            nc.tensor.matmul(arep1[:], lhsT=sel2, rhs=par[:, 512:1024], start=True, stop=True)
            cs = consts.tile([P, 2], F32, name="cs")
            nc.vector.tensor_copy(out=cs[:], in_=small[:, 0:2])
            arep0 = psum.tile([P, 512], F32, tag="acc0", name="arep0")
            nc.tensor.matmul(arep0[:], lhsT=sel2, rhs=par[:, 0:512], start=True, stop=True)
            gain = consts.tile([P, 1], F32, name="gain")
            nc.vector.tensor_scalar(
                out=gain[:], in0=cs[:, 0:1], scalar1=cs[:, 1:2], scalar2=SCALING, op0=MULT, op1=MULT
            )
            arep = [arep0, arep1]
            for g in (1, 0):
                nc.vector.scalar_tensor_tensor(
                    out=w_d[:, :, g, :],
                    in0=arep[g][:].rearrange("n (w e) -> n e w", e=2),
                    scalar=gain[:, 0:1],
                    in1=ow[:, 512 * g : 512 * (g + 1)].rearrange("n (w e) -> n e w", e=2),
                    op0=MULT,
                    op1=ADD,
                )

        def w_quantise():
            for g in (1, 0):
                wt = psum.tile([P, 4, P], BF16, tag="acc%d" % g, name="wt%d" % g)
                for u in range(2):
                    for e in range(2):
                        nc.tensor.transpose(
                            wt[:, 2 * u + e, :], w_d[:, e, g, P * u : P * (u + 1)], ident_b[:]
                        )
                nc.vector.tensor_copy(out=w_grp[:, g], in_=wt[:].rearrange("p t n -> p n t"))
            nc.vector.quantize_mx(
                out=w_codes[:].bitcast(FP8X4),
                scales=w_scl[:],
                in_=w_grp[:].rearrange("p g n t -> p (g n t)"),
            )

        banks = {}
        grps = {}
        quants = {}
        accs = {}

        def transposes(i):
            xt = psum.tile([P, 4, P], F32, tag="xt%d" % (i % XT_BANKS), name="xt")
            src, col = x_words[i]
            for q in range(4):
                nc.tensor.transpose(
                    xt[:, q, :], src[:, col + P * q : col + P * (q + 1)], ident_f[:]
                )
            banks[i] = xt

        def copy_out(i, on_vector):
            u, j = divmod(i, UNIT)
            if j == 0:
                grps[u] = gpool.tile([P, UNIT * K], BF16, tag="grp", name="grp", align_bytes=64)
            dst = grps[u][:].bitcast(F32).rearrange(
                "p (j g m u) -> p j g m u", j=UNIT, g=2, m=P, u=2
            )[:, j]
            src = banks[i][:].rearrange("p (g u) m -> p g m u", u=2)
            if on_vector:
                nc.vector.tensor_copy(out=dst, in_=src)
            else:
                nc.scalar.copy(out=dst, in_=src)

        def quantise(u):
            codes = qpool.tile([P, UNIT * 2 * P], U32, tag="codes", name="codes", align_bytes=64)
            scl = qpool.tile([P, UNIT * 2 * P], U8, tag="scl", name="scl", align_bytes=64)
            nc.vector.quantize_mx(out=codes[:].bitcast(FP8X4), scales=scl[:], in_=grps[u][:])
            quants[u] = (codes, scl)

        def products(u):
            codes, scl = quants[u]
            acc = psum.tile([P, UNIT * N_OUT], F32, tag="acc%d" % (u % 2), name="acc")
            for j in range(UNIT):
                for g in range(2):
                    cols = slice((2 * j + g) * P, (2 * j + g + 1) * P)
                    nc.tensor.matmul_mx(
                        out=acc[:, j * N_OUT : (j + 1) * N_OUT],
                        lhsT=codes[:, cols].bitcast(FP8X4),
                        lhsT_scale=scl[:, cols],
                        rhs=w_codes[:, g * P : (g + 1) * P].bitcast(FP8X4),
                        rhs_scale=w_scl[:, g * P : (g + 1) * P],
                        start=(g == 0),
                        stop=(g == 1),
                    )
            accs[u] = acc

        out_tiles = []
        first = 0
        for s, width in enumerate(STORE_GROUPS):
            ot = opool.tile([P, width * N_OUT], F32, name="o%d" % s)
            out_tiles.append((ot, first, width))
            first += width

        def results(u, on_vector):
            tile0 = UNIT * u
            for ot, first_tile, width in out_tiles:
                if first_tile <= tile0 < first_tile + width:
                    off = (tile0 - first_tile) * N_OUT
                    dst = ot[:, off : off + UNIT * N_OUT]
                    if on_vector:
                        nc.vector.tensor_copy(out=dst, in_=accs[u][:])
                    else:
                        nc.scalar.copy(out=dst, in_=accs[u][:])
                    if tile0 + UNIT == first_tile + width:
                        c_sup, t_sup = divmod(first_tile, SUPER)
                        nc.sync.dma_start(
                            out=out_v[:, c_sup, t_sup : t_sup + width, :].rearrange(
                                "p t n -> p (t n)"
                            ),
                            in_=ot[:],
                        )

        for s in range(N_GROUPS + 2):
            streaming = s < N_GROUPS
            if streaming:
                for j in range(XT_BANKS):
                    transposes(GROUP * s + j)
                    if s == 0 and j == UNIT - 1:
                        w_form()
            if 1 <= s <= N_GROUPS:
                quantise(2 * s - 1)
            if s >= 2:
                results(2 * s - 4, False)
            if streaming:
                for j in range(GROUP):
                    copy_out(GROUP * s + j, j in VECTOR_TILES)
                    if j + XT_BANKS < GROUP:
                        transposes(GROUP * s + j + XT_BANKS)
                    if j == VECTOR_TILES[0] and s >= 2:
                        results(2 * s - 3, True)
            elif s >= 2:
                results(2 * s - 3, True)
            if s == 0:
                w_quantise()
            if streaming:
                quantise(2 * s)
            if 1 <= s <= N_GROUPS:
                products(2 * s - 2)
                products(2 * s - 1)
